import numpy as np
import ml_dtypes

BF16 = ml_dtypes.bfloat16


def bf(x):
    return np.asarray(x, np.float32).astype(BF16)


def f32(x):
    return np.asarray(x, np.float32)


def f64(x):
    return np.asarray(x).astype(np.float64)


def striped(idx):
    return np.tile(idx.reshape(-1, 16).T, (8, 1))


D, S, N, WIN, SPAN = 128, 2048, 512, 128, 256
KN = N + SPAN - WIN
SCALE = D ** -0.5


def setup_inputs():
    return {"qstore": bf(1.5 * np.random.standard_normal((D, S))), "k": bf(np.random.standard_normal((D, KN))), "v": bf(np.random.standard_normal((KN, D))), "offs": striped(np.random.permutation(S)[:N])}


def reference(qstore, k, v, offs):
    idx = offs[:16].T.reshape(-1)
    q = f64(qstore)[:, idx]
    kk = f64(k)
    vv = f64(v)
    res = np.zeros((D, N), np.float64)
    for t in range(N // WIN):
        kb = kk[:, t * WIN:t * WIN + SPAN]
        vb = vv[t * WIN:t * WIN + SPAN]
        sim = SCALE * (kb.T @ q[:, t * WIN:(t + 1) * WIN])
        e = np.exp(sim)
        res[:, t * WIN:(t + 1) * WIN] = (vb.T @ e) / e.sum(axis=0, keepdims=True)
    return res

@@ -1,0 +1,85 @@
+import concourse.mybir as mybir
+from concourse.masks import make_identity
+
+BF16 = mybir.dt.bfloat16
+F32 = mybir.dt.float32
+U16 = mybir.dt.uint16
+EXP = mybir.ActivationFunctionType.Exp
+
+D = 128
+STORE = 2048
+PICKED = 512
+WIN = 128
+WINDOWS = PICKED // WIN
+BLOCKS = WINDOWS + 1
+LIST_COLS = WIN // 16
+V_PITCH = 144
+SCALE = D**-0.5
+
+FLOPS = 2 * (2 * D * 2 * WIN * PICKED)
+
+
+def tile_localattention_kernel(tc, qstore, k, v, offs, out):
+    nc = tc.nc
+    with (
+        tc.tile_pool(name="held", bufs=1) as held,
+        tc.tile_pool(name="work", bufs=2) as work,
+        tc.psum_pool(name="score_banks", bufs=1) as score_banks,
+        tc.psum_pool(name="value_banks", bufs=2) as value_banks,
+        tc.psum_pool(name="flip_banks", bufs=2) as flip_banks,
+    ):
+        offsets = held.tile([128, PICKED // 16], U16, name="offsets")
+        nc.sync.dma_start(offsets[:], offs)
+
+        keys = held.tile([D, BLOCKS * WIN], BF16, name="keys")
+        nc.scalar.dma_start(keys[:], k)
+
+        store = held.tile([D, STORE], BF16, name="store")
+        quarter = STORE // 4
+        for c in range(4):
+            queue = nc.sync if c % 2 == 0 else nc.scalar
+            queue.dma_start(store[:, c * quarter : (c + 1) * quarter], qstore[:, c * quarter : (c + 1) * quarter])
+
+        values = held.tile([WIN, BLOCKS, V_PITCH], BF16, name="values")
+        nc.sync.dma_start(values[:, :, 0:D], v.rearrange("(b p) e -> p b e", p=WIN))
+        nc.vector.memset(values[:, :, D:V_PITCH], 1.0)
+
+        identity = held.tile([128, 128], F32, name="identity")
+        make_identity(nc, identity[:])
+
+        result = held.tile([D, PICKED], F32, name="result")
+
+        scores = [score_banks.tile([WIN, 2 * WIN], F32, name=f"scores{t}") for t in range(WINDOWS)]
+        for t in range(WINDOWS):
+            picked = store[:].indirect(offsets[:, t * LIST_COLS : (t + 1) * LIST_COLS])
+            for h in range(2):
+                nc.tensor.matmul(
+                    scores[t][:, h * WIN : (h + 1) * WIN],
+                    keys[:, (t + h) * WIN : (t + h + 1) * WIN],
+                    picked,
+                    start=True,
+                    stop=True,
+                )
+
+        for t in range(WINDOWS):
+            weights = work.tile([WIN, 2 * WIN], BF16, name="weights")
+            nc.scalar.activation(weights[:], scores[t][:], EXP, scale=SCALE)
+
+            summed = value_banks.tile([WIN, D + 1], F32, name="summed")
+            for h in range(2):
+                nc.tensor.matmul(
+                    summed[:],
+                    weights[:, h * WIN : (h + 1) * WIN],
+                    values[:, t + h, 0 : D + 1],
+                    start=(h == 0),
+                    stop=(h == 1),
+                )
+            inverse = work.tile([WIN, 1], F32, name="inverse")
+            nc.vector.reciprocal(inverse[:], summed[:, D : D + 1])
+            attended = work.tile([WIN, D], F32, name="attended")
+            nc.vector.tensor_scalar_mul(attended[:], summed[:, 0:D], inverse[:])
+
+            flipped = flip_banks.tile([D, WIN], F32, name="flipped")
+            nc.tensor.transpose(flipped[:], attended[:], identity[:])
+            nc.vector.tensor_copy(result[:, t * WIN : (t + 1) * WIN], flipped[:])
+            nc.sync.dma_start(out[:, t * WIN : (t + 1) * WIN], result[:, t * WIN : (t + 1) * WIN])

@@ -14,6 +14,7 @@ WINDOWS = PICKED // WIN
 BLOCKS = WINDOWS + 1
 LIST_COLS = WIN // 16
 V_PITCH = 144
+PSUM_BANKS = 8
 SCALE = D**-0.5
 
 FLOPS = 2 * (2 * D * 2 * WIN * PICKED)
@@ -23,10 +24,8 @@ def tile_localattention_kernel(tc, qstore, k, v, offs, out):
     nc = tc.nc
     with (
         tc.tile_pool(name="held", bufs=1) as held,
-        tc.tile_pool(name="work", bufs=2) as work,
-        tc.psum_pool(name="score_banks", bufs=1) as score_banks,
-        tc.psum_pool(name="value_banks", bufs=2) as value_banks,
-        tc.psum_pool(name="flip_banks", bufs=2) as flip_banks,
+        tc.tile_pool(name="work", bufs=3) as work,
+        tc.psum_pool(name="banks", bufs=PSUM_BANKS) as banks,
     ):
         offsets = held.tile([128, PICKED // 16], U16, name="offsets")
         nc.sync.dma_start(offsets[:], offs)
@@ -49,37 +48,44 @@ def tile_localattention_kernel(tc, qstore, k, v, offs, out):
 
         result = held.tile([D, PICKED], F32, name="result")
 
-        scores = [score_banks.tile([WIN, 2 * WIN], F32, name=f"scores{t}") for t in range(WINDOWS)]
-        for t in range(WINDOWS):
-            picked = store[:].indirect(offsets[:, t * LIST_COLS : (t + 1) * LIST_COLS])
-            for h in range(2):
-                nc.tensor.matmul(
-                    scores[t][:, h * WIN : (h + 1) * WIN],
-                    keys[:, (t + h) * WIN : (t + h + 1) * WIN],
-                    picked,
-                    start=True,
-                    stop=True,
-                )
+        first = [max(b - 1, 0) for b in range(BLOCKS)]
+        users = [min(b, WINDOWS - 1) - first[b] + 1 for b in range(BLOCKS)]
+        scores = [banks.tile([WIN, 2 * WIN], F32, name=f"scores{b}", tag="bank") for b in range(BLOCKS)]
+        for b in range(BLOCKS):
+            nc.tensor.matmul(
+                scores[b][:, 0 : users[b] * WIN],
+                keys[:, b * WIN : (b + 1) * WIN],
+                store[:].indirect(offsets[:, first[b] * LIST_COLS : (first[b] + users[b]) * LIST_COLS]),
+                start=True,
+                stop=True,
+            )
 
-        for t in range(WINDOWS):
-            weights = work.tile([WIN, 2 * WIN], BF16, name="weights")
-            nc.scalar.activation(weights[:], scores[t][:], EXP, scale=SCALE)
-
-            summed = value_banks.tile([WIN, D + 1], F32, name="summed")
-            for h in range(2):
-                nc.tensor.matmul(
-                    summed[:],
-                    weights[:, h * WIN : (h + 1) * WIN],
-                    values[:, t + h, 0 : D + 1],
-                    start=(h == 0),
-                    stop=(h == 1),
-                )
-            inverse = work.tile([WIN, 1], F32, name="inverse")
-            nc.vector.reciprocal(inverse[:], summed[:, D : D + 1])
-            attended = work.tile([WIN, D], F32, name="attended")
-            nc.vector.tensor_scalar_mul(attended[:], summed[:, 0:D], inverse[:])
-
-            flipped = flip_banks.tile([D, WIN], F32, name="flipped")
-            nc.tensor.transpose(flipped[:], attended[:], identity[:])
-            nc.vector.tensor_copy(result[:, t * WIN : (t + 1) * WIN], flipped[:])
+        def flip_and_store(t):
+            flipped = banks.tile([D, 2 * WIN], F32, name="flipped", tag="bank")
+            nc.tensor.transpose(flipped[:, 0:WIN], attended[t][:], identity[:])
+            nc.scalar.copy(result[:, t * WIN : (t + 1) * WIN], flipped[:, 0:WIN])
             nc.sync.dma_start(out[:, t * WIN : (t + 1) * WIN], result[:, t * WIN : (t + 1) * WIN])
+
+        summed = [None] * WINDOWS
+        attended = [None] * WINDOWS
+        for b in range(BLOCKS):
+            weights = work.tile([WIN, users[b] * WIN], BF16, name=f"weights{users[b]}")
+            nc.scalar.activation(weights[:], scores[b][:, 0 : users[b] * WIN], EXP, scale=SCALE)
+            for t in range(first[b], first[b] + users[b]):
+                if t == b:
+                    summed[t] = banks.tile([WIN, 2 * WIN], F32, name="summed", tag="bank")
+                nc.tensor.matmul(
+                    summed[t][:, 0 : D + 1],
+                    weights[:, (t - first[b]) * WIN : (t - first[b] + 1) * WIN],
+                    values[:, b, 0 : D + 1],
+                    start=(t == b),
+                    stop=(t == b - 1),
+                )
+            if b >= 1:
+                t = b - 1
+                inverse = work.tile([WIN, 1], F32, name="inverse")
+                nc.vector.reciprocal(inverse[:], summed[t][:, D : D + 1])
+                attended[t] = work.tile([WIN, D], F32, name="attended")
+                nc.vector.tensor_scalar_mul(attended[t][:], summed[t][:, 0:D], inverse[:])
+        for t in range(WINDOWS):
+            flip_and_store(t)

@@ -34,10 +34,7 @@ def tile_localattention_kernel(tc, qstore, k, v, offs, out):
         nc.scalar.dma_start(keys[:], k)
 
         store = held.tile([D, STORE], BF16, name="store")
-        quarter = STORE // 4
-        for c in range(4):
-            queue = nc.sync if c % 2 == 0 else nc.scalar
-            queue.dma_start(store[:, c * quarter : (c + 1) * quarter], qstore[:, c * quarter : (c + 1) * quarter])
+        nc.sync.dma_start(store[:], qstore)
 
         values = held.tile([WIN, BLOCKS, V_PITCH], BF16, name="values")
         nc.sync.dma_start(values[:, :, 0:D], v.rearrange("(b p) e -> p b e", p=WIN))

@@ -24,7 +24,7 @@ def tile_localattention_kernel(tc, qstore, k, v, offs, out):
     nc = tc.nc
     with (
         tc.tile_pool(name="held", bufs=1) as held,
-        tc.tile_pool(name="work", bufs=3) as work,
+        tc.tile_pool(name="work", bufs=WINDOWS) as work,
         tc.psum_pool(name="banks", bufs=PSUM_BANKS) as banks,
     ):
         offsets = held.tile([128, PICKED // 16], U16, name="offsets")

@@ -27,17 +27,17 @@ def tile_localattention_kernel(tc, qstore, k, v, offs, out):
         tc.tile_pool(name="work", bufs=WINDOWS) as work,
         tc.psum_pool(name="banks", bufs=PSUM_BANKS) as banks,
     ):
+        store = held.tile([D, STORE], BF16, name="store")
+        nc.scalar.dma_start(store[:], qstore)
+
         offsets = held.tile([128, PICKED // 16], U16, name="offsets")
         nc.sync.dma_start(offsets[:], offs)
 
         keys = held.tile([D, BLOCKS * WIN], BF16, name="keys")
-        nc.scalar.dma_start(keys[:], k)
-
-        store = held.tile([D, STORE], BF16, name="store")
-        nc.sync.dma_start(store[:], qstore)
+        nc.sync.dma_start(keys[:], k)
 
         values = held.tile([WIN, BLOCKS, V_PITCH], BF16, name="values")
-        nc.sync.dma_start(values[:, :, 0:D], v.rearrange("(b p) e -> p b e", p=WIN))
+        nc.scalar.dma_start(values[:, :, 0:D], v.rearrange("(b p) e -> p b e", p=WIN))
         nc.vector.memset(values[:, :, D:V_PITCH], 1.0)
 
         identity = held.tile([128, 128], F32, name="identity")

@@ -28,13 +28,13 @@ def tile_localattention_kernel(tc, qstore, k, v, offs, out):
         tc.psum_pool(name="banks", bufs=PSUM_BANKS) as banks,
     ):
         store = held.tile([D, STORE], BF16, name="store")
-        nc.scalar.dma_start(store[:], qstore)
+        nc.sync.dma_start(store[:], qstore)
 
         offsets = held.tile([128, PICKED // 16], U16, name="offsets")
         nc.sync.dma_start(offsets[:], offs)
 
         keys = held.tile([D, BLOCKS * WIN], BF16, name="keys")
-        nc.sync.dma_start(keys[:], k)
+        nc.scalar.dma_start(keys[:], k)
 
         values = held.tile([WIN, BLOCKS, V_PITCH], BF16, name="values")
         nc.scalar.dma_start(values[:, :, 0:D], v.rearrange("(b p) e -> p b e", p=WIN))

import concourse.mybir as mybir
from concourse.masks import make_identity

BF16 = mybir.dt.bfloat16
F32 = mybir.dt.float32
U16 = mybir.dt.uint16
EXP = mybir.ActivationFunctionType.Exp

D = 128
STORE = 2048
PICKED = 512
WIN = 128
WINDOWS = PICKED // WIN
BLOCKS = WINDOWS + 1
LIST_COLS = WIN // 16
V_PITCH = 144
PSUM_BANKS = 8
SCALE = D**-0.5

FLOPS = 2 * (2 * D * 2 * WIN * PICKED)


def tile_localattention_kernel(tc, qstore, k, v, offs, out):
    nc = tc.nc
    with (
        tc.tile_pool(name="held", bufs=1) as held,
        tc.tile_pool(name="work", bufs=WINDOWS) as work,
        tc.psum_pool(name="banks", bufs=PSUM_BANKS) as banks,
    ):
        store = held.tile([D, STORE], BF16, name="store")
        nc.sync.dma_start(store[:], qstore)

        offsets = held.tile([128, PICKED // 16], U16, name="offsets")
        nc.sync.dma_start(offsets[:], offs)

        keys = held.tile([D, BLOCKS * WIN], BF16, name="keys")
        nc.scalar.dma_start(keys[:], k)

        values = held.tile([WIN, BLOCKS, V_PITCH], BF16, name="values")
        nc.scalar.dma_start(values[:, :, 0:D], v.rearrange("(b p) e -> p b e", p=WIN))
        nc.vector.memset(values[:, :, D:V_PITCH], 1.0)

        identity = held.tile([128, 128], F32, name="identity")
        make_identity(nc, identity[:])

        result = held.tile([D, PICKED], F32, name="result")

        first = [max(b - 1, 0) for b in range(BLOCKS)]
        users = [min(b, WINDOWS - 1) - first[b] + 1 for b in range(BLOCKS)]
        scores = [banks.tile([WIN, 2 * WIN], F32, name=f"scores{b}", tag="bank") for b in range(BLOCKS)]
        for b in range(BLOCKS):
            nc.tensor.matmul(
                scores[b][:, 0 : users[b] * WIN],
                keys[:, b * WIN : (b + 1) * WIN],
                store[:].indirect(offsets[:, first[b] * LIST_COLS : (first[b] + users[b]) * LIST_COLS]),
                start=True,
                stop=True,
            )

        def flip_and_store(t):
            flipped = banks.tile([D, 2 * WIN], F32, name="flipped", tag="bank")
            nc.tensor.transpose(flipped[:, 0:WIN], attended[t][:], identity[:])
            nc.scalar.copy(result[:, t * WIN : (t + 1) * WIN], flipped[:, 0:WIN])
            nc.sync.dma_start(out[:, t * WIN : (t + 1) * WIN], result[:, t * WIN : (t + 1) * WIN])

        summed = [None] * WINDOWS
        attended = [None] * WINDOWS
        for b in range(BLOCKS):
            weights = work.tile([WIN, users[b] * WIN], BF16, name=f"weights{users[b]}")
            nc.scalar.activation(weights[:], scores[b][:, 0 : users[b] * WIN], EXP, scale=SCALE)
            for t in range(first[b], first[b] + users[b]):
                if t == b:
                    summed[t] = banks.tile([WIN, 2 * WIN], F32, name="summed", tag="bank")
                nc.tensor.matmul(
                    summed[t][:, 0 : D + 1],
                    weights[:, (t - first[b]) * WIN : (t - first[b] + 1) * WIN],
                    values[:, b, 0 : D + 1],
                    start=(t == b),
                    stop=(t == b - 1),
                )
            if b >= 1:
                t = b - 1
                inverse = work.tile([WIN, 1], F32, name="inverse")
                nc.vector.reciprocal(inverse[:], summed[t][:, D : D + 1])
                attended[t] = work.tile([WIN, D], F32, name="attended")
                nc.vector.tensor_scalar_mul(attended[t][:], summed[t][:, 0:D], inverse[:])
        for t in range(WINDOWS):
            flip_and_store(t)
